import numpy as np
import ml_dtypes


def mxq(x, axis, fmt="e4m3"):
    dtype, down = {"e4m3": (ml_dtypes.float8_e4m3fn, 7), "e5m2": (ml_dtypes.float8_e5m2, 14)}[fmt]
    v = np.moveaxis(np.asarray(x, np.float32).astype(ml_dtypes.bfloat16).astype(np.float64), axis, -1)
    blocks = v.reshape(v.shape[:-1] + (-1, 32))
    amax = np.abs(blocks).max(-1, keepdims=True)
    byte = np.maximum(np.where(amax > 0, np.frexp(amax)[1] - 1 + 127, 0) - down, 1)
    scale = np.exp2(byte - 127.0)
    codes = (blocks / scale).astype(np.float32).astype(dtype).astype(np.float64)
    return np.moveaxis((codes * scale).reshape(v.shape), -1, axis)


WIDE = False


def mx_kscale(k):
    if not WIDE:
        return np.ones(k)
    levels = np.array([30, -30])
    if k % 512:
        return np.exp2(np.random.permutation(np.resize(levels, k // 32))).repeat(32)
    a = np.empty((k // 512, 16))
    for p in range(k // 512):
        a[p, :8] = np.random.permutation(np.resize(levels, 8))
        for g in range(8):
            far = levels[np.abs(levels - a[p, g]) >= 10]
            a[p, g + 8] = far[np.random.randint(len(far))]
    return np.exp2(a.ravel()).repeat(32)


BF16 = ml_dtypes.bfloat16


def bf(x):
    return np.asarray(x, np.float32).astype(BF16)


def f64(x):
    return np.asarray(x).astype(np.float64)


B, T, C, E, NH, QB = 1, 1024, 1024, 1024, 4, 512
HH = E // NH // 2
RMS_EPS = 1.1920929e-07
ROPE_BASE = 10000.0


def rms_norm(u):
    return u / np.sqrt(np.mean(u * u, axis=-1, keepdims=True) + RMS_EPS)


def rotary_heads(u):
    inv_freq = (1.0 / ROPE_BASE) ** (np.arange(0, HH, 2) / HH)
    freqs = np.outer(np.arange(NH), inv_freq)
    cos = np.cos(freqs)[None, :, None, :]
    sin = np.sin(freqs)[None, :, None, :]
    u1, u2 = u[..., :HH // 2], u[..., HH // 2:]
    return np.concatenate((u1 * cos + u2 * sin, -u1 * sin + u2 * cos), axis=-1)


def setup_inputs():
    s = mx_kscale(C)
    return {"x": bf(np.random.standard_normal((B, T, C)) * s),
            "wq": bf(np.random.standard_normal((E, C)) / np.sqrt(C) / s),
            "wk": bf(np.random.standard_normal((E, C)) / np.sqrt(C) / s)}


def reference(x, wq, wk):
    xq = mxq(f64(x), 2, "e5m2")
    q = (xq @ mxq(f64(wq), 1, "e4m3").T).reshape(B, T, NH, 2, HH).transpose(0, 2, 1, 3, 4)
    k = (xq @ mxq(f64(wk), 1, "e4m3").T).reshape(B, T, NH, 2, HH).transpose(0, 2, 1, 3, 4)
    q1 = rotary_heads(rms_norm(q[..., 0, :]))
    q2 = rotary_heads(rms_norm(q[..., 1, :]))
    k1 = rotary_heads(rms_norm(k[..., 0, :]))
    k2 = rotary_heads(rms_norm(k[..., 1, :]))
    return q1, q2, k1, k2

@@ -1,0 +1,308 @@
+import math
+from contextlib import ExitStack
+
+import concourse.mybir as mybir
+from concourse.masks import make_identity
+
+F32 = mybir.dt.float32
+BF16 = mybir.dt.bfloat16
+U32 = mybir.dt.uint32
+U8 = mybir.dt.uint8
+E5M2 = mybir.dt.float8_e5m2_x4
+E4M3 = mybir.dt.float8_e4m3fn_x4
+ALU = mybir.AluOpType
+FUNC = mybir.ActivationFunctionType
+
+T, C, E, NH = 1024, 1024, 1024, 4
+HH = 128
+HALF = 64
+RMS_EPS = 1.1920929e-07
+ROPE_BASE = 10000.0
+FLOPS = 2 * T * C * 2 * E
+
+P = 128
+PASSES = 2
+TILES = T // P
+VECS = 4
+
+T_BANKS = 3
+BANKS = 8
+PROD_BUFS = 3
+OUT_BUFS = 8
+HEAD = 10
+CHUNKS = (
+    [("x", 0)]
+    + [("w", 1, v) for v in range(4)]
+    + [("x", j) for j in range(1, 6)]
+    + [("w", 2, v) for v in range(4)]
+    + [("x", 6), ("x", 7)]
+    + [("w", h, v) for h in (0, 3) for v in range(4)]
+)
+UNITS = [(h, j) for h in (1, 2) for j in range(6)] + [(1, 6), (1, 7)]
+LATE = [(2, 6), (2, 7)] + [(3, j) for j in range(8)]
+PATTERN = "rzrzrrzrzrzrzrzrzr"
+UNITS = UNITS + [LATE[PATTERN[:n].count("r")] if c == "r" else (0, PATTERN[:n].count("z")) for n, c in enumerate(PATTERN)]
+SHARED = 15
+
+
+def chunk_bank(n):
+    return n % T_BANKS
+
+
+def unit_bank(i):
+    if i < SHARED:
+        return T_BANKS + i % (BANKS - T_BANKS)
+    return (i - SHARED) % BANKS
+
+
+SINGLE=((1,0),(1,1),(3,6),(3,7))
+READY = {0: (8, 2), 2: (10, 4), 5: (14, 2), 9: (16, 4), 11: (20, 4)}
+ZACT=((0,0),(0,1),(0,3),(0,5),(0,7))
+DELAY=1
+ZL=1
+STSINGLE=((3,6),(3,7))
+
+
+def tile_differentialattention_pa_kernel(tc, x, wq, wk, out_0, out_1, out_2, out_3):
+    nc = tc.nc
+    outs = (out_0, out_1, out_2, out_3)
+    ACT, DVE, POOL = "scalar", "vector", "gpsimd"
+
+    with ExitStack() as ctx:
+        keep = ctx.enter_context(tc.tile_pool(name="keep", bufs=1))
+        work = ctx.enter_context(tc.tile_pool(name="work", bufs=2))
+        psum = ctx.enter_context(tc.psum_pool(name="psum", bufs=1))
+        ctx.enter_context(tc.manual_schedule())
+
+        x_rows = x[0].rearrange("(p j) k -> p j k", j=TILES)
+        raw = []
+        for n, chunk in enumerate(CHUNKS):
+            tile = keep.tile([P, C], BF16, name="raw%d" % n)
+            if chunk[0] == "x":
+                src = x_rows[:, chunk[1], :]
+            else:
+                row0 = chunk[1] * 2 * HH + (chunk[2] % 2) * HH
+                src = (wq, wk)[chunk[2] // 2][row0 : row0 + HH, :]
+            nc.sync.dma_start(out=tile[:], in_=src)
+            raw.append(tile)
+
+        ident = keep.tile([P, P], F32, name="ident")
+        make_identity(nc, ident[:])
+
+        freq = keep.tile([P, 2, HALF], F32, name="freq")
+        nc.vector.memset(freq[:, 1, 0:1], 1.0)
+        n = 1
+        while n < HALF:
+            nc.vector.tensor_scalar(
+                out=freq[:, 1, n : 2 * n], in0=freq[:, 1, 0:n], scalar1=(1.0 / ROPE_BASE) ** (n / HALF),
+                scalar2=None, op0=ALU.mult,
+            )
+            n *= 2
+        nc.vector.tensor_scalar(out=freq[:, 0, :], in0=freq[:, 1, :], scalar1=-1.0, scalar2=None, op0=ALU.mult)
+        trig = keep.tile([P, NH - 1, 2, 2, HALF], F32, name="trig")
+        for h in range(1, NH):
+            nc.scalar.activation(
+                out=trig[:, h - 1, 0], in_=freq[:, 1:2, :].to_broadcast([P, 2, HALF]), func=FUNC.Sin,
+                scale=-float(h), bias=math.pi / 2,
+            )
+            nc.scalar.activation(out=trig[:, h - 1, 1], in_=freq[:], func=FUNC.Sin, scale=float(h))
+
+        x_stage = keep.tile([P, TILES, PASSES, P, 4], BF16, name="x_stage", align_bytes=64)
+        x_codes = keep.tile([P, TILES, PASSES, P], U32, name="x_codes", align_bytes=64)
+        x_scales = keep.tile([P, TILES, PASSES, P], U8, name="x_scales", align_bytes=64)
+        w_stage, w_codes, w_scales = {}, {}, {}
+        for h in range(NH):
+            w_stage[h] = keep.tile([P, PASSES, VECS, HH, 4], BF16, name="w_stage%d" % h, align_bytes=64)
+            w_codes[h] = keep.tile([P, PASSES, VECS, HH], U32, name="w_codes%d" % h, align_bytes=64)
+            w_scales[h] = keep.tile([P, PASSES, VECS, HH], U8, name="w_scales%d" % h, align_bytes=64)
+        sumsq = keep.tile([P, len(UNITS), VECS], F32, name="sumsq")
+        rnorm = keep.tile([P, len(UNITS), VECS], F32, name="rnorm")
+        turned, acc, prod, result = {}, {}, {}, {}
+
+        def transpose_chunk(n):
+            turned[n] = psum.tile([P, PASSES, 2, P], F32, name="turned", tag="bank%d" % chunk_bank(n))
+            words = raw[n][:].bitcast(F32)
+            for g in range(PASSES):
+                for u in range(2):
+                    nc.tensor.transpose(turned[n][:, g, u, :], words[:, 256 * g + u : 256 * (g + 1) : 2], ident[:])
+
+        def copy_chunk(n, engine):
+            chunk = CHUNKS[n]
+            if chunk[0] == "x":
+                dst = x_stage[:, chunk[1]]
+            else:
+                dst = w_stage[chunk[1]][:, :, chunk[2]]
+            dst = dst.rearrange("p g r t -> p g (r t)").bitcast(F32).rearrange("p g (r u) -> p g r u", u=2)
+            src = turned[n][:].rearrange("p g u r -> p g r u")
+            if engine == ACT:
+                nc.scalar.copy(out=dst, in_=src)
+            else:
+                nc.vector.tensor_copy(out=dst, in_=src)
+
+        def quantize(first, count, g=None):
+            chunk = CHUNKS[first]
+            if chunk[0] == "x":
+                tiles = slice(chunk[1], chunk[1] + count)
+                nc.vector.quantize_mx(
+                    out=x_codes[:, tiles].rearrange("p j g r -> p (j g r)").bitcast(E5M2),
+                    scales=x_scales[:, tiles].rearrange("p j g r -> p (j g r)"),
+                    in_=x_stage[:, tiles].rearrange("p j g r t -> p (j g r t)"),
+                )
+            else:
+                h = chunk[1]
+                passes = slice(0, PASSES) if g is None else slice(g, g + 1)
+                vecs = slice(chunk[2], chunk[2] + count)
+                nc.vector.quantize_mx(
+                    out=w_codes[h][:, passes, vecs].rearrange("p g v r -> p (g v r)").bitcast(E4M3),
+                    scales=w_scales[h][:, passes, vecs].rearrange("p g v r -> p (g v r)"),
+                    in_=w_stage[h][:, passes, vecs].rearrange("p g v r t -> p (g v r t)"),
+                )
+
+        def multiply(i):
+            h, j = UNITS[i]
+            acc[i] = psum.tile([P, VECS, HH], F32, name="acc", tag="bank%d" % unit_bank(i))
+            for g in range(PASSES):
+                nc.tensor.matmul_mx(
+                    out=acc[i][:].rearrange("p v f -> p (v f)"),
+                    lhsT=x_codes[:, j, g].bitcast(E5M2),
+                    lhsT_scale=x_scales[:, j, g],
+                    rhs=w_codes[h][:, g].rearrange("p v r -> p (v r)").bitcast(E4M3),
+                    rhs_scale=w_scales[h][:, g].rearrange("p v r -> p (v r)"),
+                    start=(g == 0),
+                    stop=(g == PASSES - 1),
+                )
+
+        def squares(i):
+            squared = work.tile([P, VECS, HH], F32, name="squared", bufs=3)
+            for v in range(VECS):
+                nc.scalar.activation(
+                    out=squared[:, v], in_=acc[i][:, v], func=FUNC.Square, accum_out=sumsq[:, i, v : v + 1]
+                )
+
+        def rstd(first, count):
+            nc.scalar.activation(
+                out=rnorm[:, first : first + count], in_=sumsq[:, first : first + count],
+                func=FUNC.Abs_reciprocal_sqrt, scale=1.0 / HH, bias=RMS_EPS,
+            )
+
+        def result_tile(h, j):
+            if (h, j // 2) not in result:
+                result[h, j // 2] = work.tile([P, VECS, 2, HH], F32, name="result", bufs=OUT_BUFS)
+            return result[h, j // 2]
+
+        def products(i, engine=DVE):
+            h, j = UNITS[i]
+            if h == 0:
+                dst = result_tile(h, j)
+                if engine == DVE:
+                    nc.vector.tensor_tensor(
+                        out=dst[:, :, j % 2, :], in0=acc[i][:],
+                        in1=rnorm[:, i, :].unsqueeze(2).to_broadcast([P, VECS, HH]), op=ALU.mult,
+                    )
+                else:
+                    for v in range(VECS):
+                        nc.scalar.activation(
+                            out=dst[:, v, j % 2, :], in_=acc[i][:, v], func=FUNC.Copy, scale=rnorm[:, i, v : v + 1]
+                        )
+                return
+            if (h, j // 2) not in prod:
+                prod[h, j // 2] = work.tile([P, VECS, 2, 2, HH], F32, name="prod", bufs=PROD_BUFS)
+            for v in range(VECS):
+                nc.vector.scalar_tensor_tensor(
+                    out=prod[h, j // 2][:, v, j % 2],
+                    in0=acc[i][:, v : v + 1, :].to_broadcast([P, 2, HH]),
+                    scalar=rnorm[:, i, v : v + 1],
+                    in1=trig[:, h - 1].rearrange("p s a f -> p s (a f)"),
+                    op0=ALU.mult,
+                    op1=ALU.mult,
+                )
+
+        def add_halves(h, j0, count, engine=POOL):
+            dst = result_tile(h, j0)
+            src = prod[h, j0 // 2]
+            tiles = slice(j0 % 2, j0 % 2 + count)
+            for a in range(2):
+                here = slice(a * HALF, (a + 1) * HALF)
+                other = slice((1 - a) * HALF, (2 - a) * HALF)
+                (nc.gpsimd if engine == POOL else nc.vector).tensor_tensor(
+                    out=dst[:, :, tiles, here], in0=src[:, :, tiles, 0, here], in1=src[:, :, tiles, 1, other], op=ALU.add
+                )
+
+        def store(h, j0, count=2):
+            for v in range(VECS):
+                rows = outs[v][0, h].rearrange("(p j) f -> p j f", j=TILES)
+                nc.sync.dma_start(out=rows[:, j0 : j0 + count, :], in_=result[h, j0 // 2][:, v, j0 % 2 : j0 % 2 + count])
+
+        transpose_chunk(0)
+        copy_chunk(0, DVE)
+        transpose_chunk(1)
+        copy_chunk(1, ACT)
+        transpose_chunk(2)
+        copy_chunk(2, DVE)
+        quantize(0, 1)
+        quantize(1, 2, 0)
+        quantize(1, 2, 1)
+        transpose_chunk(3)
+        copy_chunk(3, ACT)
+        transpose_chunk(4)
+        copy_chunk(4, ACT)
+        transpose_chunk(5)
+        copy_chunk(5, ACT)
+        quantize(3, 2, 0)
+        quantize(3, 2, 1)
+        transpose_chunk(6)
+        quantize(5, 1)
+        copy_chunk(6, DVE)
+        transpose_chunk(7)
+        copy_chunk(7, ACT)
+        transpose_chunk(8)
+        multiply(0)
+        transpose_chunk(9)
+        multiply(1)
+        copy_chunk(8, DVE)
+        quantize(6, 2)
+        copy_chunk(9, DVE)
+        squares(0)
+        rstd(0, 1)
+        transpose_chunk(10)
+        multiply(2)
+        last = len(UNITS) - 1
+        squares(1)
+        copy_chunk(10, ACT)
+        transpose_chunk(11)
+        rstd(1, 1)
+        squares(2)
+        copy_chunk(11, ACT)
+        due = {}
+        for i in range(len(UNITS)):
+            n = HEAD + i + 2
+            h, j = UNITS[i]
+            if (h, j) not in ZACT:
+                products(i)
+            if n < len(CHUNKS):
+                transpose_chunk(n)
+            if i + 3 <= last:
+                multiply(i + 3)
+            if n < len(CHUNKS):
+                copy_chunk(n, ACT)
+                rstd(i + 2, 1)
+                squares(i + 3)
+            else:
+                if i + 3 <= last:
+                    squares(i + 3)
+                if i + 2 <= last:
+                    rstd(i + 2, 1)
+            if i + ZL <= last and UNITS[i + ZL] in ZACT:
+                products(i + ZL, ACT)
+            if i in READY:
+                quantize(*READY[i])
+            if (h, j) in SINGLE:
+                add_halves(h, j, 1, DVE if (h, j) == (3, 7) else POOL)
+            elif h != 0 and j % 2 == 1:
+                add_halves(h, j - 1, 2)
+            if (h, j) in STSINGLE:
+                due.setdefault(min(i + (0 if h == 0 else DELAY), last), []).append((h, j, 1))
+            elif j % 2 == 1:
+                due.setdefault(min(i + (0 if h == 0 else DELAY), last), []).append((h, j - 1))
+            for pair in due.get(i, []):
+                store(*pair)

@@ -40,7 +40,7 @@ CHUNKS = (
 )
 UNITS = [(h, j) for h in (1, 2) for j in range(6)] + [(1, 6), (1, 7)]
 LATE = [(2, 6), (2, 7)] + [(3, j) for j in range(8)]
-PATTERN = "rzrzrrzrzrzrzrzrzr"
+PATTERN = "rzrzrrzrrzrzrzrrzz"
 UNITS = UNITS + [LATE[PATTERN[:n].count("r")] if c == "r" else (0, PATTERN[:n].count("z")) for n, c in enumerate(PATTERN)]
 SHARED = 15
 
@@ -57,10 +57,13 @@ def unit_bank(i):
 
 SINGLE=((1,0),(1,1),(3,6),(3,7))
 READY = {0: (8, 2), 2: (10, 4), 5: (14, 2), 9: (16, 4), 11: (20, 4)}
-ZACT=((0,0),(0,1),(0,3),(0,5),(0,7))
-DELAY=1
-ZL=1
+ZACT=((0,0),(0,6),(0,7))
+DELAY=3
+ZL=0
 STSINGLE=((3,6),(3,7))
+CDVE=()
+RG = {i: (i, 1) for i in (2, 3, 30, 31)}
+RG = {**RG, **{i + 1: (i, 2) for i in range(4, 30, 2)}}
 
 
 def tile_differentialattention_pa_kernel(tc, x, wq, wk, out_0, out_1, out_2, out_3):
@@ -221,12 +224,12 @@ def tile_differentialattention_pa_kernel(tc, x, wq, wk, out_0, out_1, out_2, out
             dst = result_tile(h, j0)
             src = prod[h, j0 // 2]
             tiles = slice(j0 % 2, j0 % 2 + count)
-            for a in range(2):
-                here = slice(a * HALF, (a + 1) * HALF)
-                other = slice((1 - a) * HALF, (2 - a) * HALF)
-                (nc.gpsimd if engine == POOL else nc.vector).tensor_tensor(
-                    out=dst[:, :, tiles, here], in0=src[:, :, tiles, 0, here], in1=src[:, :, tiles, 1, other], op=ALU.add
-                )
+            (nc.gpsimd if engine == POOL else nc.vector).tensor_tensor(
+                out=dst[:, :, tiles, :].rearrange("p v j (a f) -> p v j a f", a=2),
+                in0=src[:, :, tiles, 0, :].rearrange("p v j (a f) -> p v j a f", a=2),
+                in1=src[:, :, tiles, 1, :].rearrange("p v j (a f) -> p v j a f", a=2)[:, :, :, ::-1, :],
+                op=ALU.add,
+            )
 
         def store(h, j0, count=2):
             for v in range(VECS):
@@ -255,24 +258,24 @@ def tile_differentialattention_pa_kernel(tc, x, wq, wk, out_0, out_1, out_2, out
         copy_chunk(6, DVE)
         transpose_chunk(7)
         copy_chunk(7, ACT)
-        transpose_chunk(8)
         multiply(0)
-        transpose_chunk(9)
         multiply(1)
-        copy_chunk(8, DVE)
+        transpose_chunk(8)
+        transpose_chunk(9)
         quantize(6, 2)
+        copy_chunk(8, DVE)
         copy_chunk(9, DVE)
         squares(0)
-        rstd(0, 1)
-        transpose_chunk(10)
-        multiply(2)
-        last = len(UNITS) - 1
         squares(1)
-        copy_chunk(10, ACT)
+        rstd(0, 1)
+        multiply(2)
+        transpose_chunk(10)
         transpose_chunk(11)
         rstd(1, 1)
         squares(2)
+        copy_chunk(10, ACT)
         copy_chunk(11, ACT)
+        last = len(UNITS) - 1
         due = {}
         for i in range(len(UNITS)):
             n = HEAD + i + 2
@@ -284,14 +287,13 @@ def tile_differentialattention_pa_kernel(tc, x, wq, wk, out_0, out_1, out_2, out
             if i + 3 <= last:
                 multiply(i + 3)
             if n < len(CHUNKS):
-                copy_chunk(n, ACT)
-                rstd(i + 2, 1)
+                copy_chunk(n, DVE if n in CDVE else ACT)
+            elif i + 3 <= last:
                 squares(i + 3)
-            else:
-                if i + 3 <= last:
-                    squares(i + 3)
-                if i + 2 <= last:
-                    rstd(i + 2, 1)
+            if i + 2 in RG:
+                rstd(*RG[i + 2])
+            if n < len(CHUNKS):
+                squares(i + 3)
             if i + ZL <= last and UNITS[i + ZL] in ZACT:
                 products(i + ZL, ACT)
             if i in READY:
@@ -304,5 +306,5 @@ def tile_differentialattention_pa_kernel(tc, x, wq, wk, out_0, out_1, out_2, out
                 due.setdefault(min(i + (0 if h == 0 else DELAY), last), []).append((h, j, 1))
             elif j % 2 == 1:
                 due.setdefault(min(i + (0 if h == 0 else DELAY), last), []).append((h, j - 1))
-            for pair in due.get(i, []):
+            for pair in sorted(due.get(i, [])):
                 store(*pair)

@@ -110,6 +110,9 @@ def tile_differentialattention_pa_kernel(tc, x, wq, wk, out_0, out_1, out_2, out
             )
             nc.scalar.activation(out=trig[:, h - 1, 1], in_=freq[:], func=FUNC.Sin, scale=float(h))
 
+        warm = keep.tile([P, 1], F32, name="warm")
+        nc.scalar.activation(out=warm[:], in_=freq[:, 1, 0:1], func=FUNC.Abs_reciprocal_sqrt)
+
         x_stage = keep.tile([P, TILES, PASSES, P, 4], BF16, name="x_stage", align_bytes=64)
         x_codes = keep.tile([P, TILES, PASSES, P], U32, name="x_codes", align_bytes=64)
         x_scales = keep.tile([P, TILES, PASSES, P], U8, name="x_scales", align_bytes=64)

@@ -21,55 +21,40 @@ ROPE_BASE = 10000.0
 FLOPS = 2 * T * C * 2 * E
 
 P = 128
-PASSES = 2
+K_PASS = 512
+PASSES = C // K_PASS
 TILES = T // P
-VECS = 4
+OUTS = 4
+WORDS = K_PASS // 2
 
-T_BANKS = 3
-BANKS = 8
-PROD_BUFS = 3
-OUT_BUFS = 8
-HEAD = 10
-CHUNKS = (
+PIECES = (
     [("x", 0)]
-    + [("w", 1, v) for v in range(4)]
-    + [("x", j) for j in range(1, 6)]
-    + [("w", 2, v) for v in range(4)]
-    + [("x", 6), ("x", 7)]
-    + [("w", h, v) for h in (0, 3) for v in range(4)]
+    + [("w", 0, g, pair) for g in range(PASSES) for pair in range(2)]
+    + [("x", j) for j in range(1, TILES)]
+    + [("w", v, g, pair) for v in range(1, OUTS) for g in range(PASSES) for pair in range(2)]
 )
-UNITS = [(h, j) for h in (1, 2) for j in range(6)] + [(1, 6), (1, 7)]
-LATE = [(2, 6), (2, 7)] + [(3, j) for j in range(8)]
-PATTERN = "rzrzrrzrrzrzrzrrzz"
-UNITS = UNITS + [LATE[PATTERN[:n].count("r")] if c == "r" else (0, PATTERN[:n].count("z")) for n, c in enumerate(PATTERN)]
-SHARED = 15
+PRODUCTS = OUTS * TILES
+STEPS = PRODUCTS // 2
+TURN_BANKS = 3
+SUM_BANKS = 5
+HEAD = 7
+QUANT_LAG = 3
+REORDERED = 12
+FAST_STEPS = 3
+SINGLE_HEAD = 2
+SINGLE_TAIL = 3
 
 
-def chunk_bank(n):
-    return n % T_BANKS
-
-
-def unit_bank(i):
-    if i < SHARED:
-        return T_BANKS + i % (BANKS - T_BANKS)
-    return (i - SHARED) % BANKS
-
-
-SINGLE=((1,0),(1,1),(3,6),(3,7))
-READY = {0: (8, 2), 2: (10, 4), 5: (14, 2), 9: (16, 4), 11: (20, 4)}
-ZACT=((0,0),(0,6),(0,7))
-DELAY=3
-ZL=0
-STSINGLE=((3,6),(3,7))
-CDVE=()
-RG = {i: (i, 1) for i in (2, 3, 30, 31)}
-RG = {**RG, **{i + 1: (i, 2) for i in range(4, 30, 2)}}
+def pieces_of_step(s):
+    fast = min(s + 1, FAST_STEPS)
+    first = HEAD + TURN_BANKS * fast + (s + 1 - fast)
+    count = TURN_BANKS if s + 1 < FAST_STEPS else 1
+    return [n for n in range(first, first + count) if n < len(PIECES)]
 
 
 def tile_differentialattention_pa_kernel(tc, x, wq, wk, out_0, out_1, out_2, out_3):
     nc = tc.nc
     outs = (out_0, out_1, out_2, out_3)
-    ACT, DVE, POOL = "scalar", "vector", "gpsimd"
 
     with ExitStack() as ctx:
         keep = ctx.enter_context(tc.tile_pool(name="keep", bufs=1))
@@ -77,15 +62,16 @@ def tile_differentialattention_pa_kernel(tc, x, wq, wk, out_0, out_1, out_2, out
         psum = ctx.enter_context(tc.psum_pool(name="psum", bufs=1))
         ctx.enter_context(tc.manual_schedule())
 
-        x_rows = x[0].rearrange("(p j) k -> p j k", j=TILES)
+        x_rows = x[0].rearrange("(p j) (g k) -> p j g k", j=TILES, g=PASSES)
         raw = []
-        for n, chunk in enumerate(CHUNKS):
-            tile = keep.tile([P, C], BF16, name="raw%d" % n)
-            if chunk[0] == "x":
-                src = x_rows[:, chunk[1], :]
+        for n, piece in enumerate(PIECES):
+            tile = keep.tile([P, 2, K_PASS], BF16, name="raw%d" % n)
+            if piece[0] == "x":
+                src = x_rows[:, piece[1]]
             else:
-                row0 = chunk[1] * 2 * HH + (chunk[2] % 2) * HH
-                src = (wq, wk)[chunk[2] // 2][row0 : row0 + HH, :]
+                v, g, pair = piece[1:]
+                w_rows = (wq, wk)[v // 2].rearrange("(h a p) k -> p h a k", a=2, p=HH)
+                src = w_rows[:, 2 * pair : 2 * pair + 2, v % 2, g * K_PASS : (g + 1) * K_PASS]
             nc.sync.dma_start(out=tile[:], in_=src)
             raw.append(tile)
 
@@ -116,198 +102,194 @@ def tile_differentialattention_pa_kernel(tc, x, wq, wk, out_0, out_1, out_2, out
         x_stage = keep.tile([P, TILES, PASSES, P, 4], BF16, name="x_stage", align_bytes=64)
         x_codes = keep.tile([P, TILES, PASSES, P], U32, name="x_codes", align_bytes=64)
         x_scales = keep.tile([P, TILES, PASSES, P], U8, name="x_scales", align_bytes=64)
-        w_stage, w_codes, w_scales = {}, {}, {}
-        for h in range(NH):
-            w_stage[h] = keep.tile([P, PASSES, VECS, HH, 4], BF16, name="w_stage%d" % h, align_bytes=64)
-            w_codes[h] = keep.tile([P, PASSES, VECS, HH], U32, name="w_codes%d" % h, align_bytes=64)
-            w_scales[h] = keep.tile([P, PASSES, VECS, HH], U8, name="w_scales%d" % h, align_bytes=64)
-        sumsq = keep.tile([P, len(UNITS), VECS], F32, name="sumsq")
-        rnorm = keep.tile([P, len(UNITS), VECS], F32, name="rnorm")
-        turned, acc, prod, result = {}, {}, {}, {}
+        w_stage = keep.tile([P, OUTS * PASSES * 2, 2, HH, 4], BF16, name="w_stage", align_bytes=64)
+        w_codes = keep.tile([P, OUTS * PASSES * 2, 2, HH], U32, name="w_codes", align_bytes=64)
+        w_scales = keep.tile([P, OUTS * PASSES * 2, 2, HH], U8, name="w_scales", align_bytes=64)
+        sumsq = keep.tile([P, PRODUCTS, NH], F32, name="sumsq")
+        rnorm = keep.tile([P, PRODUCTS, NH], F32, name="rnorm")
+        ordered, turned, acc, prod, result = {}, {}, {}, {}, {}
 
-        def transpose_chunk(n):
-            turned[n] = psum.tile([P, PASSES, 2, P], F32, name="turned", tag="bank%d" % chunk_bank(n))
+        def place(n):
+            piece = PIECES[n]
+            if piece[0] == "x":
+                return x_stage, x_codes, x_scales, E5M2, piece[1]
+            v, g, pair = piece[1:]
+            return w_stage, w_codes, w_scales, E4M3, (v * PASSES + g) * 2 + pair
+
+        def reorder(n):
+            ordered[n] = work.tile([P, 2, 2, P], F32, name="ordered", bufs=6)
             words = raw[n][:].bitcast(F32)
-            for g in range(PASSES):
+            nc.vector.tensor_copy(out=ordered[n][:], in_=words.rearrange("p e (r u) -> p e u r", u=2))
+
+        def turn(n):
+            turned[n] = psum.tile([P, 2, 2, P], F32, name="turned", tag="bank%d" % (n % TURN_BANKS))
+            words = raw[n][:].bitcast(F32)
+            for e in range(2):
                 for u in range(2):
-                    nc.tensor.transpose(turned[n][:, g, u, :], words[:, 256 * g + u : 256 * (g + 1) : 2], ident[:])
+                    src = ordered[n][:, e, u, :] if n in ordered else words[:, e, u:WORDS:2]
+                    nc.tensor.transpose(turned[n][:, e, u, :], src, ident[:])
 
-        def copy_chunk(n, engine):
-            chunk = CHUNKS[n]
-            if chunk[0] == "x":
-                dst = x_stage[:, chunk[1]]
-            else:
-                dst = w_stage[chunk[1]][:, :, chunk[2]]
-            dst = dst.rearrange("p g r t -> p g (r t)").bitcast(F32).rearrange("p g (r u) -> p g r u", u=2)
-            src = turned[n][:].rearrange("p g u r -> p g r u")
-            if engine == ACT:
-                nc.scalar.copy(out=dst, in_=src)
-            else:
+        def copy_out(n, on_vector=False):
+            stage, slot = place(n)[0], place(n)[4]
+            dst = stage[:, slot].rearrange("p e r t -> p e (r t)").bitcast(F32).rearrange("p e (r u) -> p e r u", u=2)
+            src = turned[n][:].rearrange("p e u r -> p e r u")
+            if on_vector:
                 nc.vector.tensor_copy(out=dst, in_=src)
-
-        def quantize(first, count, g=None):
-            chunk = CHUNKS[first]
-            if chunk[0] == "x":
-                tiles = slice(chunk[1], chunk[1] + count)
-                nc.vector.quantize_mx(
-                    out=x_codes[:, tiles].rearrange("p j g r -> p (j g r)").bitcast(E5M2),
-                    scales=x_scales[:, tiles].rearrange("p j g r -> p (j g r)"),
-                    in_=x_stage[:, tiles].rearrange("p j g r t -> p (j g r t)"),
-                )
             else:
-                h = chunk[1]
-                passes = slice(0, PASSES) if g is None else slice(g, g + 1)
-                vecs = slice(chunk[2], chunk[2] + count)
-                nc.vector.quantize_mx(
-                    out=w_codes[h][:, passes, vecs].rearrange("p g v r -> p (g v r)").bitcast(E4M3),
-                    scales=w_scales[h][:, passes, vecs].rearrange("p g v r -> p (g v r)"),
-                    in_=w_stage[h][:, passes, vecs].rearrange("p g v r t -> p (g v r t)"),
-                )
+                nc.scalar.copy(out=dst, in_=src)
+
+        def quantize(first, count):
+            stage, codes, scales, dtype, slot = place(first)
+            slots = slice(slot, slot + count)
+            nc.vector.quantize_mx(
+                out=codes[:, slots].rearrange("p n e r -> p (n e r)").bitcast(dtype),
+                scales=scales[:, slots].rearrange("p n e r -> p (n e r)"),
+                in_=stage[:, slots].rearrange("p n e r t -> p (n e r t)"),
+            )
 
         def multiply(i):
-            h, j = UNITS[i]
-            acc[i] = psum.tile([P, VECS, HH], F32, name="acc", tag="bank%d" % unit_bank(i))
+            v, j = divmod(i, TILES)
+            acc[i] = psum.tile([P, NH, HH], F32, name="acc", tag="bank%d" % (TURN_BANKS + i % SUM_BANKS))
             for g in range(PASSES):
+                slots = slice((v * PASSES + g) * 2, (v * PASSES + g) * 2 + 2)
                 nc.tensor.matmul_mx(
-                    out=acc[i][:].rearrange("p v f -> p (v f)"),
+                    out=acc[i][:].rearrange("p h f -> p (h f)"),
                     lhsT=x_codes[:, j, g].bitcast(E5M2),
                     lhsT_scale=x_scales[:, j, g],
-                    rhs=w_codes[h][:, g].rearrange("p v r -> p (v r)").bitcast(E4M3),
-                    rhs_scale=w_scales[h][:, g].rearrange("p v r -> p (v r)"),
+                    rhs=w_codes[:, slots].rearrange("p n e r -> p (n e r)").bitcast(E4M3),
+                    rhs_scale=w_scales[:, slots].rearrange("p n e r -> p (n e r)"),
                     start=(g == 0),
                     stop=(g == PASSES - 1),
                 )
 
         def squares(i):
-            squared = work.tile([P, VECS, HH], F32, name="squared", bufs=3)
-            for v in range(VECS):
+            squared = work.tile([P, NH, HH], F32, name="squared", bufs=3)
+            for h in range(NH):
                 nc.scalar.activation(
-                    out=squared[:, v], in_=acc[i][:, v], func=FUNC.Square, accum_out=sumsq[:, i, v : v + 1]
+                    out=squared[:, h], in_=acc[i][:, h], func=FUNC.Square, accum_out=sumsq[:, i, h : h + 1]
                 )
 
-        def rstd(first, count):
+        def norm_factors(first):
             nc.scalar.activation(
-                out=rnorm[:, first : first + count], in_=sumsq[:, first : first + count],
+                out=rnorm[:, first : first + 2], in_=sumsq[:, first : first + 2],
                 func=FUNC.Abs_reciprocal_sqrt, scale=1.0 / HH, bias=RMS_EPS,
             )
 
-        def result_tile(h, j):
-            if (h, j // 2) not in result:
-                result[h, j // 2] = work.tile([P, VECS, 2, HH], F32, name="result", bufs=OUT_BUFS)
-            return result[h, j // 2]
+        def result_tile(i):
+            if i // 2 not in result:
+                result[i // 2] = work.tile([P, NH, 2, HH], F32, name="result", bufs=4)
+            return result[i // 2]
 
-        def products(i, engine=DVE):
-            h, j = UNITS[i]
-            if h == 0:
-                dst = result_tile(h, j)
-                if engine == DVE:
-                    nc.vector.tensor_tensor(
-                        out=dst[:, :, j % 2, :], in0=acc[i][:],
-                        in1=rnorm[:, i, :].unsqueeze(2).to_broadcast([P, VECS, HH]), op=ALU.mult,
-                    )
-                else:
-                    for v in range(VECS):
-                        nc.scalar.activation(
-                            out=dst[:, v, j % 2, :], in_=acc[i][:, v], func=FUNC.Copy, scale=rnorm[:, i, v : v + 1]
-                        )
-                return
-            if (h, j // 2) not in prod:
-                prod[h, j // 2] = work.tile([P, VECS, 2, 2, HH], F32, name="prod", bufs=PROD_BUFS)
-            for v in range(VECS):
+        def scale_head0(i, on_vector=True):
+            dst = result_tile(i)[:, 0, i % 2, :]
+            if on_vector:
+                nc.vector.tensor_scalar(
+                    out=dst, in0=acc[i][:, 0], scalar1=rnorm[:, i, 0:1], scalar2=None, op0=ALU.mult
+                )
+            else:
+                nc.scalar.activation(out=dst, in_=acc[i][:, 0], func=FUNC.Copy, scale=rnorm[:, i, 0:1])
+
+        def rotation_terms(i):
+            if i // 2 not in prod:
+                prod[i // 2] = work.tile([P, NH - 1, 2, 2, HH], F32, name="prod", bufs=3)
+            for h in range(1, NH):
                 nc.vector.scalar_tensor_tensor(
-                    out=prod[h, j // 2][:, v, j % 2],
-                    in0=acc[i][:, v : v + 1, :].to_broadcast([P, 2, HH]),
-                    scalar=rnorm[:, i, v : v + 1],
+                    out=prod[i // 2][:, h - 1, i % 2],
+                    in0=acc[i][:, h : h + 1, :].to_broadcast([P, 2, HH]),
+                    scalar=rnorm[:, i, h : h + 1],
                     in1=trig[:, h - 1].rearrange("p s a f -> p s (a f)"),
                     op0=ALU.mult,
                     op1=ALU.mult,
                 )
 
-        def add_halves(h, j0, count, engine=POOL):
-            dst = result_tile(h, j0)
-            src = prod[h, j0 // 2]
-            tiles = slice(j0 % 2, j0 % 2 + count)
-            (nc.gpsimd if engine == POOL else nc.vector).tensor_tensor(
-                out=dst[:, :, tiles, :].rearrange("p v j (a f) -> p v j a f", a=2),
-                in0=src[:, :, tiles, 0, :].rearrange("p v j (a f) -> p v j a f", a=2),
-                in1=src[:, :, tiles, 1, :].rearrange("p v j (a f) -> p v j a f", a=2)[:, :, :, ::-1, :],
+        def add_terms(first, count, on_vector=False):
+            tiles = slice(first % 2, first % 2 + count)
+            src = prod[first // 2]
+            (nc.vector if on_vector else nc.gpsimd).tensor_tensor(
+                out=result_tile(first)[:, 1:, tiles, :].rearrange("p h j (a f) -> p h j a f", a=2),
+                in0=src[:, :, tiles, 0, :].rearrange("p h j (a f) -> p h j a f", a=2),
+                in1=src[:, :, tiles, 1, :].rearrange("p h j (a f) -> p h j a f", a=2)[:, :, :, ::-1, :],
                 op=ALU.add,
             )
 
-        def store(h, j0, count=2):
-            for v in range(VECS):
-                rows = outs[v][0, h].rearrange("(p j) f -> p j f", j=TILES)
-                nc.sync.dma_start(out=rows[:, j0 : j0 + count, :], in_=result[h, j0 // 2][:, v, j0 % 2 : j0 % 2 + count])
+        def store(first, count):
+            v, j = divmod(first, TILES)
+            rows = outs[v][0].rearrange("h (p j) f -> p h j f", j=TILES)
+            nc.sync.dma_start(
+                out=rows[:, :, j : j + count, :], in_=result[first // 2][:, :, first % 2 : first % 2 + count]
+            )
 
-        transpose_chunk(0)
-        copy_chunk(0, DVE)
-        transpose_chunk(1)
-        copy_chunk(1, ACT)
-        transpose_chunk(2)
-        copy_chunk(2, DVE)
-        quantize(0, 1)
-        quantize(1, 2, 0)
-        quantize(1, 2, 1)
-        transpose_chunk(3)
-        copy_chunk(3, ACT)
-        transpose_chunk(4)
-        copy_chunk(4, ACT)
-        transpose_chunk(5)
-        copy_chunk(5, ACT)
-        quantize(3, 2, 0)
-        quantize(3, 2, 1)
-        transpose_chunk(6)
-        quantize(5, 1)
-        copy_chunk(6, DVE)
-        transpose_chunk(7)
-        copy_chunk(7, ACT)
+        for n in range(HEAD + QUANT_LAG):
+            if n < HEAD:
+                reorder(n)
+                turn(n)
+                copy_out(n)
+            if n >= QUANT_LAG:
+                quantize(n - QUANT_LAG, 1)
         multiply(0)
         multiply(1)
-        transpose_chunk(8)
-        transpose_chunk(9)
-        quantize(6, 2)
-        copy_chunk(8, DVE)
-        copy_chunk(9, DVE)
+        for n in range(HEAD, REORDERED):
+            reorder(n)
+        pieces = pieces_of_step(-1)
+        for n in pieces:
+            turn(n)
         squares(0)
         squares(1)
-        rstd(0, 1)
-        multiply(2)
-        transpose_chunk(10)
-        transpose_chunk(11)
-        rstd(1, 1)
-        squares(2)
-        copy_chunk(10, ACT)
-        copy_chunk(11, ACT)
-        last = len(UNITS) - 1
-        due = {}
-        for i in range(len(UNITS)):
-            n = HEAD + i + 2
-            h, j = UNITS[i]
-            if (h, j) not in ZACT:
-                products(i)
-            if n < len(CHUNKS):
-                transpose_chunk(n)
-            if i + 3 <= last:
-                multiply(i + 3)
-            if n < len(CHUNKS):
-                copy_chunk(n, DVE if n in CDVE else ACT)
-            elif i + 3 <= last:
-                squares(i + 3)
-            if i + 2 in RG:
-                rstd(*RG[i + 2])
-            if n < len(CHUNKS):
-                squares(i + 3)
-            if i + ZL <= last and UNITS[i + ZL] in ZACT:
-                products(i + ZL, ACT)
-            if i in READY:
-                quantize(*READY[i])
-            if (h, j) in SINGLE:
-                add_halves(h, j, 1, DVE if (h, j) == (3, 7) else POOL)
-            elif h != 0 and j % 2 == 1:
-                add_halves(h, j - 1, 2)
-            if (h, j) in STSINGLE:
-                due.setdefault(min(i + (0 if h == 0 else DELAY), last), []).append((h, j, 1))
-            elif j % 2 == 1:
-                due.setdefault(min(i + (0 if h == 0 else DELAY), last), []).append((h, j - 1))
-            for pair in sorted(due.get(i, [])):
-                store(*pair)
+        copy_out(pieces[0], on_vector=True)
+        copy_out(pieces[1])
+        norm_factors(0)
+        copy_out(pieces[2])
+        quantize(pieces[0], 1)
+        copied = pieces[-1] + 1
+        quantized = pieces[0] + 1
+
+        for s in range(STEPS):
+            a, b = 2 * s, 2 * s + 1
+            last = s == STEPS - 1
+            pieces = pieces_of_step(s)
+            by_vector = pieces[:1] if s == 0 else []
+            by_scalar = [n for n in pieces if n not in by_vector]
+            single = s < SINGLE_HEAD or s >= STEPS - SINGLE_TAIL
+            if not last:
+                multiply(a + 2)
+                multiply(b + 2)
+            for n in pieces:
+                turn(n)
+            if pieces:
+                scale_head0(a)
+            rotation_terms(a)
+            if s <= SINGLE_HEAD and quantized + 2 <= copied:
+                quantize(quantized, 2)
+                quantized += 2
+            if single:
+                add_terms(a, 1)
+            if not last:
+                squares(a + 2)
+                squares(b + 2)
+            for n in by_scalar[:1]:
+                copy_out(n)
+            if not pieces:
+                scale_head0(a, on_vector=False)
+            if not last:
+                norm_factors(a + 2)
+            for n in by_scalar[1:]:
+                copy_out(n)
+            if not by_vector:
+                copied += len(pieces)
+            scale_head0(b)
+            rotation_terms(b)
+            if quantized + 2 <= copied:
+                quantize(quantized, 2)
+                quantized += 2
+            for n in by_vector:
+                copy_out(n, on_vector=True)
+                copied += len(pieces)
+            if single:
+                add_terms(b, 1, on_vector=last)
+            else:
+                add_terms(a, 2)
+            if s >= STEPS - SINGLE_TAIL:
+                store(a, 1)
+                store(b, 1)
+            else:
+                store(a, 2)

@@ -23,9 +23,11 @@ FLOPS = 2 * T * C * 2 * E
 P = 128
 K_PASS = 512
 PASSES = C // K_PASS
+WORDS = K_PASS // 2
 TILES = T // P
 OUTS = 4
-WORDS = K_PASS // 2
+PRODUCTS = OUTS * TILES
+STEPS = PRODUCTS // 2
 
 PIECES = (
     [("x", 0)]
@@ -33,22 +35,24 @@ PIECES = (
     + [("x", j) for j in range(1, TILES)]
     + [("w", v, g, pair) for v in range(1, OUTS) for g in range(PASSES) for pair in range(2)]
 )
-PRODUCTS = OUTS * TILES
-STEPS = PRODUCTS // 2
+
+BANKS = 8
 TURN_BANKS = 3
-SUM_BANKS = 5
 HEAD = 7
 QUANT_LAG = 3
-REORDERED = 12
-FAST_STEPS = 3
-SINGLE_HEAD = 2
-SINGLE_TAIL = 3
+REORDERED = 10
+FIRST_TURNS = (3, 3, 3, 2)
+SINGLE_ADD_STEPS = 2
+ORDERED_BUFS = 6
+SQUARED_BUFS = 3
+TERM_BUFS = 3
+RESULT_BUFS = 4
 
 
 def pieces_of_step(s):
-    fast = min(s + 1, FAST_STEPS)
-    first = HEAD + TURN_BANKS * fast + (s + 1 - fast)
-    count = TURN_BANKS if s + 1 < FAST_STEPS else 1
+    listed = min(s + 1, len(FIRST_TURNS))
+    first = HEAD + sum(FIRST_TURNS[:listed]) + (s + 1 - listed)
+    count = FIRST_TURNS[s + 1] if s + 1 < len(FIRST_TURNS) else 1
     return [n for n in range(first, first + count) if n < len(PIECES)]
 
 
@@ -99,15 +103,17 @@ def tile_differentialattention_pa_kernel(tc, x, wq, wk, out_0, out_1, out_2, out
         warm = keep.tile([P, 1], F32, name="warm")
         nc.scalar.activation(out=warm[:], in_=freq[:, 1, 0:1], func=FUNC.Abs_reciprocal_sqrt)
 
+        w_pieces = OUTS * PASSES * 2
         x_stage = keep.tile([P, TILES, PASSES, P, 4], BF16, name="x_stage", align_bytes=64)
         x_codes = keep.tile([P, TILES, PASSES, P], U32, name="x_codes", align_bytes=64)
         x_scales = keep.tile([P, TILES, PASSES, P], U8, name="x_scales", align_bytes=64)
-        w_stage = keep.tile([P, OUTS * PASSES * 2, 2, HH, 4], BF16, name="w_stage", align_bytes=64)
-        w_codes = keep.tile([P, OUTS * PASSES * 2, 2, HH], U32, name="w_codes", align_bytes=64)
-        w_scales = keep.tile([P, OUTS * PASSES * 2, 2, HH], U8, name="w_scales", align_bytes=64)
+        w_stage = keep.tile([P, w_pieces, 2, HH, 4], BF16, name="w_stage", align_bytes=64)
+        w_codes = keep.tile([P, w_pieces, 2, HH], U32, name="w_codes", align_bytes=64)
+        w_scales = keep.tile([P, w_pieces, 2, HH], U8, name="w_scales", align_bytes=64)
         sumsq = keep.tile([P, PRODUCTS, NH], F32, name="sumsq")
         rnorm = keep.tile([P, PRODUCTS, NH], F32, name="rnorm")
-        ordered, turned, acc, prod, result = {}, {}, {}, {}, {}
+        ordered, turned, acc, terms, result = {}, {}, {}, {}, {}
+        product_banks = list(range(TURN_BANKS, BANKS))
 
         def place(n):
             piece = PIECES[n]
@@ -117,7 +123,7 @@ def tile_differentialattention_pa_kernel(tc, x, wq, wk, out_0, out_1, out_2, out
             return w_stage, w_codes, w_scales, E4M3, (v * PASSES + g) * 2 + pair
 
         def reorder(n):
-            ordered[n] = work.tile([P, 2, 2, P], F32, name="ordered", bufs=6)
+            ordered[n] = work.tile([P, 2, 2, P], F32, name="ordered", bufs=ORDERED_BUFS)
             words = raw[n][:].bitcast(F32)
             nc.vector.tensor_copy(out=ordered[n][:], in_=words.rearrange("p e (r u) -> p e u r", u=2))
 
@@ -130,8 +136,8 @@ def tile_differentialattention_pa_kernel(tc, x, wq, wk, out_0, out_1, out_2, out
                     nc.tensor.transpose(turned[n][:, e, u, :], src, ident[:])
 
         def copy_out(n, on_vector=False):
-            stage, slot = place(n)[0], place(n)[4]
-            dst = stage[:, slot].rearrange("p e r t -> p e (r t)").bitcast(F32).rearrange("p e (r u) -> p e r u", u=2)
+            stage, index = place(n)[0], place(n)[4]
+            dst = stage[:, index].rearrange("p e r t -> p e (r t)").bitcast(F32).rearrange("p e (r u) -> p e r u", u=2)
             src = turned[n][:].rearrange("p e u r -> p e r u")
             if on_vector:
                 nc.vector.tensor_copy(out=dst, in_=src)
@@ -139,62 +145,64 @@ def tile_differentialattention_pa_kernel(tc, x, wq, wk, out_0, out_1, out_2, out
                 nc.scalar.copy(out=dst, in_=src)
 
         def quantize(first, count):
-            stage, codes, scales, dtype, slot = place(first)
-            slots = slice(slot, slot + count)
+            stage, codes, scales, dtype, index = place(first)
+            span = slice(index, index + count)
             nc.vector.quantize_mx(
-                out=codes[:, slots].rearrange("p n e r -> p (n e r)").bitcast(dtype),
-                scales=scales[:, slots].rearrange("p n e r -> p (n e r)"),
-                in_=stage[:, slots].rearrange("p n e r t -> p (n e r t)"),
+                out=codes[:, span].rearrange("p n e r -> p (n e r)").bitcast(dtype),
+                scales=scales[:, span].rearrange("p n e r -> p (n e r)"),
+                in_=stage[:, span].rearrange("p n e r t -> p (n e r t)"),
             )
 
         def multiply(i):
             v, j = divmod(i, TILES)
-            acc[i] = psum.tile([P, NH, HH], F32, name="acc", tag="bank%d" % (TURN_BANKS + i % SUM_BANKS))
+            bank = product_banks.pop(0)
+            product_banks.append(bank)
+            acc[i] = psum.tile([P, NH, HH], F32, name="acc", tag="bank%d" % bank)
             for g in range(PASSES):
-                slots = slice((v * PASSES + g) * 2, (v * PASSES + g) * 2 + 2)
+                span = slice((v * PASSES + g) * 2, (v * PASSES + g) * 2 + 2)
                 nc.tensor.matmul_mx(
                     out=acc[i][:].rearrange("p h f -> p (h f)"),
                     lhsT=x_codes[:, j, g].bitcast(E5M2),
                     lhsT_scale=x_scales[:, j, g],
-                    rhs=w_codes[:, slots].rearrange("p n e r -> p (n e r)").bitcast(E4M3),
-                    rhs_scale=w_scales[:, slots].rearrange("p n e r -> p (n e r)"),
+                    rhs=w_codes[:, span].rearrange("p n e r -> p (n e r)").bitcast(E4M3),
+                    rhs_scale=w_scales[:, span].rearrange("p n e r -> p (n e r)"),
                     start=(g == 0),
                     stop=(g == PASSES - 1),
                 )
 
         def squares(i):
-            squared = work.tile([P, NH, HH], F32, name="squared", bufs=3)
+            squared = work.tile([P, NH, HH], F32, name="squared", bufs=SQUARED_BUFS)
             for h in range(NH):
                 nc.scalar.activation(
                     out=squared[:, h], in_=acc[i][:, h], func=FUNC.Square, accum_out=sumsq[:, i, h : h + 1]
                 )
 
-        def norm_factors(first):
+        def norm_factors(first, count):
             nc.scalar.activation(
-                out=rnorm[:, first : first + 2], in_=sumsq[:, first : first + 2],
+                out=rnorm[:, first : first + count], in_=sumsq[:, first : first + count],
                 func=FUNC.Abs_reciprocal_sqrt, scale=1.0 / HH, bias=RMS_EPS,
             )
 
         def result_tile(i):
             if i // 2 not in result:
-                result[i // 2] = work.tile([P, NH, 2, HH], F32, name="result", bufs=4)
+                result[i // 2] = work.tile([P, NH, 2, HH], F32, name="result", bufs=RESULT_BUFS)
             return result[i // 2]
 
         def scale_head0(i, on_vector=True):
             dst = result_tile(i)[:, 0, i % 2, :]
             if on_vector:
-                nc.vector.tensor_scalar(
-                    out=dst, in0=acc[i][:, 0], scalar1=rnorm[:, i, 0:1], scalar2=None, op0=ALU.mult
+                nc.vector.tensor_tensor(
+                    out=dst, in0=acc[i][:, 0], in1=rnorm[:, i, 0:1].to_broadcast([P, HH]), op=ALU.mult
                 )
             else:
                 nc.scalar.activation(out=dst, in_=acc[i][:, 0], func=FUNC.Copy, scale=rnorm[:, i, 0:1])
 
         def rotation_terms(i):
-            if i // 2 not in prod:
-                prod[i // 2] = work.tile([P, NH - 1, 2, 2, HH], F32, name="prod", bufs=3)
+            if i // 2 not in terms:
+                terms[i // 2] = work.tile([P, NH - 1, 2, 2, HH], F32, name="terms", bufs=TERM_BUFS)
             for h in range(1, NH):
                 nc.vector.scalar_tensor_tensor(
-                    out=prod[i // 2][:, h - 1, i % 2],
+                    out=terms[i // 2][:, h - 1, i % 2],
                     in0=acc[i][:, h : h + 1, :].to_broadcast([P, 2, HH]),
                     scalar=rnorm[:, i, h : h + 1],
                     in1=trig[:, h - 1].rearrange("p s a f -> p s (a f)"),
@@ -204,7 +212,7 @@ def tile_differentialattention_pa_kernel(tc, x, wq, wk, out_0, out_1, out_2, out
 
         def add_terms(first, count, on_vector=False):
             tiles = slice(first % 2, first % 2 + count)
-            src = prod[first // 2]
+            src = terms[first // 2]
             (nc.vector if on_vector else nc.gpsimd).tensor_tensor(
                 out=result_tile(first)[:, 1:, tiles, :].rearrange("p h j (a f) -> p h j a f", a=2),
                 in0=src[:, :, tiles, 0, :].rearrange("p h j (a f) -> p h j a f", a=2),
@@ -230,39 +238,46 @@ def tile_differentialattention_pa_kernel(tc, x, wq, wk, out_0, out_1, out_2, out
         multiply(1)
         for n in range(HEAD, REORDERED):
             reorder(n)
+
         pieces = pieces_of_step(-1)
         for n in pieces:
             turn(n)
         squares(0)
-        squares(1)
         copy_out(pieces[0], on_vector=True)
-        copy_out(pieces[1])
-        norm_factors(0)
-        copy_out(pieces[2])
+        norm_factors(0, 1)
+        squares(1)
+        for n in pieces[1:]:
+            copy_out(n)
+        norm_factors(1, 1)
         quantize(pieces[0], 1)
-        copied = pieces[-1] + 1
         quantized = pieces[0] + 1
+        ready = pieces[-1] + 1
 
         for s in range(STEPS):
             a, b = 2 * s, 2 * s + 1
             last = s == STEPS - 1
             pieces = pieces_of_step(s)
             by_vector = pieces[:1] if s == 0 else []
-            by_scalar = [n for n in pieces if n not in by_vector]
-            single = s < SINGLE_HEAD or s >= STEPS - SINGLE_TAIL
+            by_scalar = pieces[len(by_vector) :]
+            single = s < SINGLE_ADD_STEPS or s == STEPS - 2
+
+            if pieces_of_step(s - 1) and not pieces:
+                product_banks[0:0] = range(TURN_BANKS)
             if not last:
                 multiply(a + 2)
                 multiply(b + 2)
             for n in pieces:
                 turn(n)
+
             if pieces:
                 scale_head0(a)
             rotation_terms(a)
-            if s <= SINGLE_HEAD and quantized + 2 <= copied:
+            if s <= SINGLE_ADD_STEPS:
                 quantize(quantized, 2)
                 quantized += 2
             if single:
                 add_terms(a, 1)
+
             if not last:
                 squares(a + 2)
                 squares(b + 2)
@@ -271,24 +286,24 @@ def tile_differentialattention_pa_kernel(tc, x, wq, wk, out_0, out_1, out_2, out
             if not pieces:
                 scale_head0(a, on_vector=False)
             if not last:
-                norm_factors(a + 2)
+                norm_factors(a + 2, 2)
             for n in by_scalar[1:]:
                 copy_out(n)
-            if not by_vector:
-                copied += len(pieces)
+
             scale_head0(b)
             rotation_terms(b)
-            if quantized + 2 <= copied:
+            if quantized + 2 <= ready + (1 if s == 1 else 0):
                 quantize(quantized, 2)
                 quantized += 2
             for n in by_vector:
                 copy_out(n, on_vector=True)
-                copied += len(pieces)
+            ready += len(pieces)
+
             if single:
-                add_terms(b, 1, on_vector=last)
+                add_terms(b, 1)
             else:
-                add_terms(a, 2)
-            if s >= STEPS - SINGLE_TAIL:
+                add_terms(a, 2, on_vector=last)
+            if s == STEPS - 2:
                 store(a, 1)
                 store(b, 1)
             else:

import math
from contextlib import ExitStack

import concourse.mybir as mybir
from concourse.masks import make_identity

F32 = mybir.dt.float32
BF16 = mybir.dt.bfloat16
U32 = mybir.dt.uint32
U8 = mybir.dt.uint8
E5M2 = mybir.dt.float8_e5m2_x4
E4M3 = mybir.dt.float8_e4m3fn_x4
ALU = mybir.AluOpType
FUNC = mybir.ActivationFunctionType

T, C, E, NH = 1024, 1024, 1024, 4
HH = 128
HALF = 64
RMS_EPS = 1.1920929e-07
ROPE_BASE = 10000.0
FLOPS = 2 * T * C * 2 * E

P = 128
K_PASS = 512
PASSES = C // K_PASS
WORDS = K_PASS // 2
TILES = T // P
OUTS = 4
PRODUCTS = OUTS * TILES
STEPS = PRODUCTS // 2

PIECES = (
    [("x", 0)]
    + [("w", 0, g, pair) for g in range(PASSES) for pair in range(2)]
    + [("x", j) for j in range(1, TILES)]
    + [("w", v, g, pair) for v in range(1, OUTS) for g in range(PASSES) for pair in range(2)]
)

BANKS = 8
TURN_BANKS = 3
HEAD = 7
QUANT_LAG = 3
REORDERED = 10
FIRST_TURNS = (3, 3, 3, 2)
SINGLE_ADD_STEPS = 2
ORDERED_BUFS = 6
SQUARED_BUFS = 3
TERM_BUFS = 3
RESULT_BUFS = 4


def pieces_of_step(s):
    listed = min(s + 1, len(FIRST_TURNS))
    first = HEAD + sum(FIRST_TURNS[:listed]) + (s + 1 - listed)
    count = FIRST_TURNS[s + 1] if s + 1 < len(FIRST_TURNS) else 1
    return [n for n in range(first, first + count) if n < len(PIECES)]


def tile_differentialattention_pa_kernel(tc, x, wq, wk, out_0, out_1, out_2, out_3):
    nc = tc.nc
    outs = (out_0, out_1, out_2, out_3)

    with ExitStack() as ctx:
        keep = ctx.enter_context(tc.tile_pool(name="keep", bufs=1))
        work = ctx.enter_context(tc.tile_pool(name="work", bufs=2))
        psum = ctx.enter_context(tc.psum_pool(name="psum", bufs=1))
        ctx.enter_context(tc.manual_schedule())

        x_rows = x[0].rearrange("(p j) (g k) -> p j g k", j=TILES, g=PASSES)
        raw = []
        for n, piece in enumerate(PIECES):
            tile = keep.tile([P, 2, K_PASS], BF16, name="raw%d" % n)
            if piece[0] == "x":
                src = x_rows[:, piece[1]]
            else:
                v, g, pair = piece[1:]
                w_rows = (wq, wk)[v // 2].rearrange("(h a p) k -> p h a k", a=2, p=HH)
                src = w_rows[:, 2 * pair : 2 * pair + 2, v % 2, g * K_PASS : (g + 1) * K_PASS]
            nc.sync.dma_start(out=tile[:], in_=src)
            raw.append(tile)

        ident = keep.tile([P, P], F32, name="ident")
        make_identity(nc, ident[:])

        freq = keep.tile([P, 2, HALF], F32, name="freq")
        nc.vector.memset(freq[:, 1, 0:1], 1.0)
        n = 1
        while n < HALF:
            nc.vector.tensor_scalar(
                out=freq[:, 1, n : 2 * n], in0=freq[:, 1, 0:n], scalar1=(1.0 / ROPE_BASE) ** (n / HALF),
                scalar2=None, op0=ALU.mult,
            )
            n *= 2
        nc.vector.tensor_scalar(out=freq[:, 0, :], in0=freq[:, 1, :], scalar1=-1.0, scalar2=None, op0=ALU.mult)
        trig = keep.tile([P, NH - 1, 2, 2, HALF], F32, name="trig")
        for h in range(1, NH):
            nc.scalar.activation(
                out=trig[:, h - 1, 0], in_=freq[:, 1:2, :].to_broadcast([P, 2, HALF]), func=FUNC.Sin,
                scale=-float(h), bias=math.pi / 2,
            )
            nc.scalar.activation(out=trig[:, h - 1, 1], in_=freq[:], func=FUNC.Sin, scale=float(h))

        warm = keep.tile([P, 1], F32, name="warm")
        nc.scalar.activation(out=warm[:], in_=freq[:, 1, 0:1], func=FUNC.Abs_reciprocal_sqrt)

        w_pieces = OUTS * PASSES * 2
        x_stage = keep.tile([P, TILES, PASSES, P, 4], BF16, name="x_stage", align_bytes=64)
        x_codes = keep.tile([P, TILES, PASSES, P], U32, name="x_codes", align_bytes=64)
        x_scales = keep.tile([P, TILES, PASSES, P], U8, name="x_scales", align_bytes=64)
        w_stage = keep.tile([P, w_pieces, 2, HH, 4], BF16, name="w_stage", align_bytes=64)
        w_codes = keep.tile([P, w_pieces, 2, HH], U32, name="w_codes", align_bytes=64)
        w_scales = keep.tile([P, w_pieces, 2, HH], U8, name="w_scales", align_bytes=64)
        sumsq = keep.tile([P, PRODUCTS, NH], F32, name="sumsq")
        rnorm = keep.tile([P, PRODUCTS, NH], F32, name="rnorm")
        ordered, turned, acc, terms, result = {}, {}, {}, {}, {}
        product_banks = list(range(TURN_BANKS, BANKS))

        def place(n):
            piece = PIECES[n]
            if piece[0] == "x":
                return x_stage, x_codes, x_scales, E5M2, piece[1]
            v, g, pair = piece[1:]
            return w_stage, w_codes, w_scales, E4M3, (v * PASSES + g) * 2 + pair

        def reorder(n):
            ordered[n] = work.tile([P, 2, 2, P], F32, name="ordered", bufs=ORDERED_BUFS)
            words = raw[n][:].bitcast(F32)
            nc.vector.tensor_copy(out=ordered[n][:], in_=words.rearrange("p e (r u) -> p e u r", u=2))

        def turn(n):
            turned[n] = psum.tile([P, 2, 2, P], F32, name="turned", tag="bank%d" % (n % TURN_BANKS))
            words = raw[n][:].bitcast(F32)
            for e in range(2):
                for u in range(2):
                    src = ordered[n][:, e, u, :] if n in ordered else words[:, e, u:WORDS:2]
                    nc.tensor.transpose(turned[n][:, e, u, :], src, ident[:])

        def copy_out(n, on_vector=False):
            stage, index = place(n)[0], place(n)[4]
            dst = stage[:, index].rearrange("p e r t -> p e (r t)").bitcast(F32).rearrange("p e (r u) -> p e r u", u=2)
            src = turned[n][:].rearrange("p e u r -> p e r u")
            if on_vector:
                nc.vector.tensor_copy(out=dst, in_=src)
            else:
                nc.scalar.copy(out=dst, in_=src)

        def quantize(first, count):
            stage, codes, scales, dtype, index = place(first)
            span = slice(index, index + count)
            nc.vector.quantize_mx(
                out=codes[:, span].rearrange("p n e r -> p (n e r)").bitcast(dtype),
                scales=scales[:, span].rearrange("p n e r -> p (n e r)"),
                in_=stage[:, span].rearrange("p n e r t -> p (n e r t)"),
            )

        def multiply(i):
            v, j = divmod(i, TILES)
            bank = product_banks.pop(0)
            product_banks.append(bank)
            acc[i] = psum.tile([P, NH, HH], F32, name="acc", tag="bank%d" % bank)
            for g in range(PASSES):
                span = slice((v * PASSES + g) * 2, (v * PASSES + g) * 2 + 2)
                nc.tensor.matmul_mx(
                    out=acc[i][:].rearrange("p h f -> p (h f)"),
                    lhsT=x_codes[:, j, g].bitcast(E5M2),
                    lhsT_scale=x_scales[:, j, g],
                    rhs=w_codes[:, span].rearrange("p n e r -> p (n e r)").bitcast(E4M3),
                    rhs_scale=w_scales[:, span].rearrange("p n e r -> p (n e r)"),
                    start=(g == 0),
                    stop=(g == PASSES - 1),
                )

        def squares(i):
            squared = work.tile([P, NH, HH], F32, name="squared", bufs=SQUARED_BUFS)
            for h in range(NH):
                nc.scalar.activation(
                    out=squared[:, h], in_=acc[i][:, h], func=FUNC.Square, accum_out=sumsq[:, i, h : h + 1]
                )

        def norm_factors(first, count):
            nc.scalar.activation(
                out=rnorm[:, first : first + count], in_=sumsq[:, first : first + count],
                func=FUNC.Abs_reciprocal_sqrt, scale=1.0 / HH, bias=RMS_EPS,
            )

        def result_tile(i):
            if i // 2 not in result:
                result[i // 2] = work.tile([P, NH, 2, HH], F32, name="result", bufs=RESULT_BUFS)
            return result[i // 2]

        def scale_head0(i, on_vector=True):
            dst = result_tile(i)[:, 0, i % 2, :]
            if on_vector:
                nc.vector.tensor_tensor(
                    out=dst, in0=acc[i][:, 0], in1=rnorm[:, i, 0:1].to_broadcast([P, HH]), op=ALU.mult
                )
            else:
                nc.scalar.activation(out=dst, in_=acc[i][:, 0], func=FUNC.Copy, scale=rnorm[:, i, 0:1])

        def rotation_terms(i):
            if i // 2 not in terms:
                terms[i // 2] = work.tile([P, NH - 1, 2, 2, HH], F32, name="terms", bufs=TERM_BUFS)
            for h in range(1, NH):
                nc.vector.scalar_tensor_tensor(
                    out=terms[i // 2][:, h - 1, i % 2],
                    in0=acc[i][:, h : h + 1, :].to_broadcast([P, 2, HH]),
                    scalar=rnorm[:, i, h : h + 1],
                    in1=trig[:, h - 1].rearrange("p s a f -> p s (a f)"),
                    op0=ALU.mult,
                    op1=ALU.mult,
                )

        def add_terms(first, count, on_vector=False):
            tiles = slice(first % 2, first % 2 + count)
            src = terms[first // 2]
            (nc.vector if on_vector else nc.gpsimd).tensor_tensor(
                out=result_tile(first)[:, 1:, tiles, :].rearrange("p h j (a f) -> p h j a f", a=2),
                in0=src[:, :, tiles, 0, :].rearrange("p h j (a f) -> p h j a f", a=2),
                in1=src[:, :, tiles, 1, :].rearrange("p h j (a f) -> p h j a f", a=2)[:, :, :, ::-1, :],
                op=ALU.add,
            )

        def store(first, count):
            v, j = divmod(first, TILES)
            rows = outs[v][0].rearrange("h (p j) f -> p h j f", j=TILES)
            nc.sync.dma_start(
                out=rows[:, :, j : j + count, :], in_=result[first // 2][:, :, first % 2 : first % 2 + count]
            )

        for n in range(HEAD + QUANT_LAG):
            if n < HEAD:
                reorder(n)
                turn(n)
                copy_out(n)
            if n >= QUANT_LAG:
                quantize(n - QUANT_LAG, 1)
        multiply(0)
        multiply(1)
        for n in range(HEAD, REORDERED):
            reorder(n)

        pieces = pieces_of_step(-1)
        for n in pieces:
            turn(n)
        squares(0)
        copy_out(pieces[0], on_vector=True)
        norm_factors(0, 1)
        squares(1)
        for n in pieces[1:]:
            copy_out(n)
        norm_factors(1, 1)
        quantize(pieces[0], 1)
        quantized = pieces[0] + 1
        ready = pieces[-1] + 1

        for s in range(STEPS):
            a, b = 2 * s, 2 * s + 1
            last = s == STEPS - 1
            pieces = pieces_of_step(s)
            by_vector = pieces[:1] if s == 0 else []
            by_scalar = pieces[len(by_vector) :]
            single = s < SINGLE_ADD_STEPS or s == STEPS - 2

            if pieces_of_step(s - 1) and not pieces:
                product_banks[0:0] = range(TURN_BANKS)
            if not last:
                multiply(a + 2)
                multiply(b + 2)
            for n in pieces:
                turn(n)

            if pieces:
                scale_head0(a)
            rotation_terms(a)
            if s <= SINGLE_ADD_STEPS:
                quantize(quantized, 2)
                quantized += 2
            if single:
                add_terms(a, 1)

            if not last:
                squares(a + 2)
                squares(b + 2)
            for n in by_scalar[:1]:
                copy_out(n)
            if not pieces:
                scale_head0(a, on_vector=False)
            if not last:
                norm_factors(a + 2, 2)
            for n in by_scalar[1:]:
                copy_out(n)

            scale_head0(b)
            rotation_terms(b)
            if quantized + 2 <= ready + (1 if s == 1 else 0):
                quantize(quantized, 2)
                quantized += 2
            for n in by_vector:
                copy_out(n, on_vector=True)
            ready += len(pieces)

            if single:
                add_terms(b, 1)
            else:
                add_terms(a, 2, on_vector=last)
            if s == STEPS - 2:
                store(a, 1)
                store(b, 1)
            else:
                store(a, 2)
